import numpy as np
import ml_dtypes


def mxq(x, axis, fmt="e4m3"):
    dtype, down = {"e4m3": (ml_dtypes.float8_e4m3fn, 7), "e5m2": (ml_dtypes.float8_e5m2, 14)}[fmt]
    v = np.moveaxis(np.asarray(x, np.float32).astype(ml_dtypes.bfloat16).astype(np.float64), axis, -1)
    blocks = v.reshape(v.shape[:-1] + (-1, 32))
    amax = np.abs(blocks).max(-1, keepdims=True)
    byte = np.maximum(np.where(amax > 0, np.frexp(amax)[1] - 1 + 127, 0) - down, 1)
    scale = np.exp2(byte - 127.0)
    codes = (blocks / scale).astype(np.float32).astype(dtype).astype(np.float64)
    return np.moveaxis((codes * scale).reshape(v.shape), -1, axis)


WIDE = False


def mx_kscale(k):
    if not WIDE:
        return np.ones(k)
    levels = np.array([20, -20, 10, -10, 0])
    a = np.random.permutation(np.resize(levels, k // 512 * 4)).reshape(k // 512, 4)
    idx = np.arange(k)
    return np.exp2(a[idx // 512, idx % 128 // 32])


BF16 = ml_dtypes.bfloat16


def bf(x):
    return np.asarray(x, np.float32).astype(BF16)


def f64(x):
    return np.asarray(x).astype(np.float64)


T, B, I, H = 16, 128, 512, 1024


def sigmoid(v):
    return 1.0 / (1.0 + np.exp(-v))


def setup_inputs():
    u = mx_kscale(H)
    u3 = np.tile(u, 3)
    x = bf(np.random.standard_normal((T, B, I)))
    w0 = bf(np.random.standard_normal((3 * H, I)) / np.sqrt(I))
    b = bf(np.random.standard_normal(3 * H) * 0.3)
    gh = bf(np.random.standard_normal((B, 3 * H)) * 0.5)
    g = bf(np.random.standard_normal((B, T, H)) * np.exp2(np.random.randint(-12, 1, (B, T, 1))) * 32.0 * u)
    gi = f64(x) @ f64(w0).T + f64(b)
    return {"input_seq": x,
            "W_ih": bf(f64(w0) / u3[:, None]),
            "b_ih": b,
            "gh": gh,
            "gi": np.asarray(gi, np.float32),
            "grad_out": g}


def reference(input_seq, W_ih, b_ih, gh, gi, grad_out):
    a = f64(gi)
    g = f64(gh)
    dh = np.transpose(f64(grad_out), (1, 0, 2))
    h_n = g[:, 2 * H:]
    r = sigmoid(a[..., :H] + g[:, :H])
    z = sigmoid(a[..., H:2 * H] + g[:, H:2 * H])
    n = np.tanh(a[..., 2 * H:] + r * h_n)
    d_n = dh * (1.0 - z) * (1.0 - n * n)
    d_z = -dh * n * z * (1.0 - z)
    d_r = d_n * h_n * r * (1.0 - r)
    dgi = np.concatenate([d_r, d_z, d_n], axis=-1)
    return mxq(dgi, 2, "e5m2") @ mxq(f64(W_ih), 0, "e4m3")

@@ -1,0 +1,230 @@
+from contextlib import ExitStack
+
+import concourse.mybir as mybir
+from concourse.masks import make_identity
+
+F32 = mybir.dt.float32
+BF16 = mybir.dt.bfloat16
+U32 = mybir.dt.uint32
+U8 = mybir.dt.uint8
+E4M3X4 = mybir.dt.float8_e4m3fn_x4
+E5M2X4 = mybir.dt.float8_e5m2_x4
+ALU = mybir.AluOpType
+FUNC = mybir.ActivationFunctionType
+
+T = 16
+B = 128
+I = 512
+H = 1024
+P = 128
+PACK = 4
+K_PASS = P * PACK
+HALVES = H // K_PASS
+GATES = 3
+PASSES = GATES * HALVES
+BLOCKS = H // P
+
+FLOPS = 2 * T * B * GATES * H * I
+BYTES = 4 * T * B * GATES * H + 2 * B * T * H + 2 * B * GATES * H + 2 * GATES * H * I + 4 * T * B * I
+
+
+def tile_grucellmodel_pa_v_kernel(tc, input_seq, W_ih, b_ih, gh, gi, grad_out, out):
+    nc = tc.nc
+    with ExitStack() as pools:
+        const = pools.enter_context(tc.tile_pool(name="const", bufs=1))
+        w_stage = pools.enter_context(tc.tile_pool(name="w_stage", bufs=2))
+        gi_pool = pools.enter_context(tc.tile_pool(name="gi", bufs=3))
+        work = pools.enter_context(tc.tile_pool(name="work", bufs=3))
+        quant = pools.enter_context(tc.tile_pool(name="quant", bufs=2))
+        result = pools.enter_context(tc.tile_pool(name="result", bufs=2))
+        psum_fixed = pools.enter_context(tc.psum_pool(name="psum_fixed", bufs=1))
+        psum_x = pools.enter_context(tc.psum_pool(name="psum_x", bufs=3))
+        psum_an = pools.enter_context(tc.psum_pool(name="psum_an", bufs=2))
+
+        gh_sb = const.tile([P, GATES * H], BF16)
+        nc.sync.dma_start(out=gh_sb[:], in_=gh)
+        gi_tiles = {}
+
+        def load_gi(t):
+            gi_t = gi_pool.tile([P, GATES * H], F32, name="gi_t")
+            nc.sync.dma_start(out=gi_t[:], in_=gi[t])
+            gi_tiles[t] = gi_t
+
+        load_gi(0)
+        go_sb = const.tile([P, T, H], BF16)
+        GO_CHUNK = 4
+        nc.sync.dma_start(out=go_sb[:, 0:GO_CHUNK, :], in_=grad_out[:, 0:GO_CHUNK, :])
+
+        ident_f32 = const.tile([P, P], F32)
+        make_identity(nc, ident_f32[:])
+        ident_bf16 = const.tile([P, P], BF16)
+        make_identity(nc, ident_bf16[:])
+        minus_half = const.tile([P, 1], F32)
+        nc.vector.memset(minus_half[:], -0.5)
+
+        g_rz = const.tile([P, 2 * H], F32)
+        nc.vector.tensor_copy(out=g_rz[:], in_=gh_sb[:, 0 : 2 * H])
+        neg_hn = const.tile([P, H], BF16)
+        nc.vector.tensor_scalar(
+            out=neg_hn[:], in0=gh_sb[:, 2 * H : 3 * H], scalar1=-1.0, scalar2=None, op0=ALU.mult
+        )
+        neg_hn_t = psum_fixed.tile([P, BLOCKS, B], BF16)
+        for blk in range(BLOCKS):
+            nc.tensor.transpose(neg_hn_t[:, blk, :], neg_hn[:, blk * P : (blk + 1) * P], ident_bf16[:])
+
+        w_codes = const.tile([P, PASSES, I], U32, align_bytes=64)
+        w_scales = const.tile([P, PASSES, I], U8, align_bytes=64)
+        w_view = W_ih.rearrange("(g j p) n -> g p j n", j=PACK, p=P)
+        w_grouped = {}
+
+        def group_w(g):
+            w_raw = w_stage.tile([P, PACK, I], BF16, name="w_raw")
+            nc.sync.dma_start(out=w_raw[:], in_=w_view[g])
+            w_grp = w_stage.tile([P, I, PACK], BF16, name="w_grp", align_bytes=64)
+            nc.vector.tensor_copy(
+                out=w_grp[:].rearrange("p (c i) j -> p c j i", i=4),
+                in_=w_raw[:].rearrange("p j (c i) -> p c j i", i=4),
+            )
+            w_grouped[g] = w_grp
+
+        def quantise_w(g):
+            nc.vector.quantize_mx(
+                out=w_codes[:, g, :].bitcast(E4M3X4),
+                scales=w_scales[:, g, :],
+                in_=w_grouped[g][:].rearrange("p n j -> p (n j)"),
+            )
+
+        group_w(0)
+        for g in range(1, PASSES):
+            group_w(g)
+            quantise_w(g - 1)
+        quantise_w(PASSES - 1)
+
+        live = {}
+
+        def by_token(flat, half):
+            return flat[:, half * K_PASS : (half + 1) * K_PASS].rearrange("p (b j) -> p b j", j=PACK)
+
+        def gates_r_z(t):
+            gi_t = gi_tiles[t]
+            r = work.tile([P, H], F32, name="r")
+            z = work.tile([P, H], F32, name="z")
+            for gate, dst in ((0, r), (1, z)):
+                for half in range(HALVES):
+                    x = psum_x.tile([P, PACK, B], F32, name="x")
+                    for j in range(PACK):
+                        cols = slice(gate * H + half * K_PASS + j * P, gate * H + half * K_PASS + (j + 1) * P)
+                        nc.tensor.matmul(
+                            x[:, j, :], lhsT=gi_t[:, cols], rhs=ident_f32[:],
+                            is_transpose=True, start=True, stop=False,
+                        )
+                        nc.tensor.matmul(
+                            x[:, j, :], lhsT=g_rz[:, cols], rhs=ident_f32[:],
+                            is_transpose=True, start=False, stop=True,
+                        )
+                    nc.scalar.activation(
+                        out=by_token(dst, half), in_=x[:].rearrange("p j b -> p b j"), func=FUNC.Sigmoid
+                    )
+            sr = work.tile([P, H], F32, name="sr")
+            nc.scalar.activation(out=sr[:], in_=r[:], func=FUNC.Square, bias=minus_half[:], scale=1.0)
+            live[t] = {"r": r, "z": z, "sr": sr}
+
+        def gate_n(t):
+            gi_t = gi_tiles[t]
+            tiles = live[t]
+            a_n = []
+            for half in range(HALVES):
+                a_half = psum_an.tile([P, PACK, B], F32, name="a_half")
+                for j in range(PACK):
+                    cols = slice(2 * H + half * K_PASS + j * P, 2 * H + half * K_PASS + (j + 1) * P)
+                    nc.tensor.transpose(a_half[:, j, :], gi_t[:, cols], ident_f32[:])
+                a_n.append(a_half)
+            dh_t = psum_fixed.tile([P, BLOCKS, B], BF16, name="dh_t")
+            for blk in range(BLOCKS):
+                nc.tensor.transpose(dh_t[:, blk, :], go_sb[:, t, blk * P : (blk + 1) * P], ident_bf16[:])
+
+            n = work.tile([P, H], F32, name="n")
+            nc.vector.tensor_tensor(
+                out=n[:].rearrange("p (h b j) -> p h b j", h=HALVES, j=PACK),
+                in0=tiles["r"][:].rearrange("p (h b j) -> p h b j", h=HALVES, j=PACK),
+                in1=neg_hn_t[:].rearrange("p (h j) b -> p h b j", h=HALVES),
+                op=ALU.mult,
+            )
+            q = work.tile([P, H], F32, name="q")
+            for half in range(HALVES):
+                blocks = slice(half * PACK, (half + 1) * PACK)
+                nc.vector.tensor_tensor(
+                    out=by_token(n, half), in0=a_n[half][:].rearrange("p j b -> p b j"),
+                    in1=by_token(n, half), op=ALU.subtract,
+                )
+                nc.vector.scalar_tensor_tensor(
+                    out=by_token(q, half), in0=by_token(tiles["z"], half), scalar=1.0,
+                    in1=dh_t[:, blocks, :].rearrange("p j b -> p b j"), op0=ALU.subtract, op1=ALU.mult,
+                )
+                nc.vector.scalar_tensor_tensor(
+                    out=by_token(tiles["sr"], half), in0=by_token(tiles["sr"], half), scalar=0.25,
+                    in1=neg_hn_t[:, blocks, :].rearrange("p j b -> p b j"), op0=ALU.subtract, op1=ALU.mult,
+                )
+            nc.scalar.activation(out=n[:], in_=n[:], func=FUNC.Tanh)
+            sn = work.tile([P, H], F32, name="sn")
+            nc.scalar.activation(out=sn[:], in_=n[:], func=FUNC.Square)
+            tiles["n"] = n
+            tiles["q"] = q
+            tiles["sn"] = sn
+
+        def gradients(t):
+            tiles = live[t]
+            dgi = quant.tile([P, GATES, H], BF16, name="dgi", align_bytes=64)
+            nc.vector.scalar_tensor_tensor(
+                out=tiles["sn"][:], in0=tiles["sn"][:], scalar=1.0, in1=tiles["q"][:],
+                op0=ALU.subtract, op1=ALU.mult,
+            )
+            nc.vector.tensor_tensor(out=tiles["n"][:], in0=tiles["n"][:], in1=tiles["z"][:], op=ALU.mult)
+            nc.scalar.copy(out=dgi[:, 2, :], in_=tiles["sn"][:])
+            nc.gpsimd.tensor_tensor(out=dgi[:, 1, :], in0=tiles["n"][:], in1=tiles["q"][:], op=ALU.mult)
+            nc.gpsimd.tensor_tensor(out=dgi[:, 0, :], in0=tiles["sr"][:], in1=tiles["sn"][:], op=ALU.mult)
+            tiles["dgi"] = dgi
+
+        def quantise(t):
+            tiles = live[t]
+            codes = quant.tile([P, GATES, H // PACK], U32, name="codes", align_bytes=64)
+            scales = quant.tile([P, GATES, H // PACK], U8, name="scales", align_bytes=64)
+            for gate in (2, 1, 0):
+                nc.vector.quantize_mx(
+                    out=codes[:, gate, :].bitcast(E5M2X4), scales=scales[:, gate, :], in_=tiles["dgi"][:, gate, :]
+                )
+            tiles["codes"] = codes
+            tiles["scales"] = scales
+
+        def multiply(t):
+            tiles = live[t]
+            acc = psum_fixed.tile([B, I], F32, name="acc")
+            for g in range(PASSES):
+                gate, half = divmod(g, HALVES)
+                tokens = slice(half * B, (half + 1) * B)
+                nc.tensor.matmul_mx(
+                    out=acc[:],
+                    lhsT=tiles["codes"][:, gate, tokens].bitcast(E5M2X4),
+                    lhsT_scale=tiles["scales"][:, gate, tokens],
+                    rhs=w_codes[:, g, :].bitcast(E4M3X4),
+                    rhs_scale=w_scales[:, g, :],
+                    start=(g == 0),
+                    stop=(g == PASSES - 1),
+                )
+            o_sb = result.tile([B, I], F32, name="o_sb")
+            nc.scalar.copy(out=o_sb[:], in_=acc[:])
+            nc.sync.dma_start(out=out[t], in_=o_sb[:])
+
+        STAGES = (gates_r_z, gate_n, gradients, quantise, multiply)
+        for step in range(T + len(STAGES) - 1):
+            ahead = step + 1
+            if ahead < T:
+                load_gi(ahead)
+                if ahead % GO_CHUNK == 0:
+                    nc.sync.dma_start(
+                        out=go_sb[:, ahead : ahead + GO_CHUNK, :], in_=grad_out[:, ahead : ahead + GO_CHUNK, :]
+                    )
+            for lag, stage in enumerate(STAGES):
+                t = step - lag
+                if 0 <= t < T:
+                    stage(t)

@@ -152,11 +152,12 @@ def tile_grucellmodel_pa_v_kernel(tc, input_seq, W_ih, b_ih, gh, gi, grad_out, o
             )
             q = work.tile([P, H], F32, name="q")
             for half in range(HALVES):
-                blocks = slice(half * PACK, (half + 1) * PACK)
                 nc.vector.tensor_tensor(
                     out=by_token(n, half), in0=a_n[half][:].rearrange("p j b -> p b j"),
                     in1=by_token(n, half), op=ALU.subtract,
                 )
+            for half in range(HALVES):
+                blocks = slice(half * PACK, (half + 1) * PACK)
                 nc.vector.scalar_tensor_tensor(
                     out=by_token(q, half), in0=by_token(tiles["z"], half), scalar=1.0,
                     in1=dh_t[:, blocks, :].rearrange("p j b -> p b j"), op0=ALU.subtract, op1=ALU.mult,
@@ -215,16 +216,17 @@ def tile_grucellmodel_pa_v_kernel(tc, input_seq, W_ih, b_ih, gh, gi, grad_out, o
             nc.scalar.copy(out=o_sb[:], in_=acc[:])
             nc.sync.dma_start(out=out[t], in_=o_sb[:])
 
-        STAGES = (gates_r_z, gate_n, gradients, quantise, multiply)
-        for step in range(T + len(STAGES) - 1):
-            ahead = step + 1
-            if ahead < T:
-                load_gi(ahead)
-                if ahead % GO_CHUNK == 0:
-                    nc.sync.dma_start(
-                        out=go_sb[:, ahead : ahead + GO_CHUNK, :], in_=grad_out[:, ahead : ahead + GO_CHUNK, :]
-                    )
-            for lag, stage in enumerate(STAGES):
-                t = step - lag
-                if 0 <= t < T:
-                    stage(t)
+        STAGES = ((quantise, 3), (multiply, 3), (gradients, 2), (gate_n, 1), (gates_r_z, 0))
+        with tc.manual_schedule(engines={mybir.EngineType.DVE, mybir.EngineType.Pool}):
+            for step in range(T + 3):
+                ahead = step + 1
+                if ahead < T:
+                    load_gi(ahead)
+                    if ahead % GO_CHUNK == 0:
+                        nc.sync.dma_start(
+                            out=go_sb[:, ahead : ahead + GO_CHUNK, :], in_=grad_out[:, ahead : ahead + GO_CHUNK, :]
+                        )
+                for stage, lag in STAGES:
+                    t = step - lag
+                    if 0 <= t < T:
+                        stage(t)

@@ -216,7 +216,7 @@ def tile_grucellmodel_pa_v_kernel(tc, input_seq, W_ih, b_ih, gh, gi, grad_out, o
             nc.scalar.copy(out=o_sb[:], in_=acc[:])
             nc.sync.dma_start(out=out[t], in_=o_sb[:])
 
-        STAGES = ((quantise, 3), (multiply, 3), (gradients, 2), (gate_n, 1), (gates_r_z, 0))
+        STAGES = ((gradients, 2), (gate_n, 1), (quantise, 3), (multiply, 3), (gates_r_z, 0))
         with tc.manual_schedule(engines={mybir.EngineType.DVE, mybir.EngineType.Pool}):
             for step in range(T + 3):
                 ahead = step + 1

@@ -22,7 +22,7 @@ K_PASS = P * PACK
 HALVES = H // K_PASS
 GATES = 3
 PASSES = GATES * HALVES
-BLOCKS = H // P
+GATE_ORDER = (1, 2, 0)
 
 FLOPS = 2 * T * B * GATES * H * I
 BYTES = 4 * T * B * GATES * H + 2 * B * T * H + 2 * B * GATES * H + 2 * GATES * H * I + 4 * T * B * I
@@ -32,6 +32,7 @@ def tile_grucellmodel_pa_v_kernel(tc, input_seq, W_ih, b_ih, gh, gi, grad_out, o
     nc = tc.nc
     with ExitStack() as pools:
         const = pools.enter_context(tc.tile_pool(name="const", bufs=1))
+        w_load = pools.enter_context(tc.tile_pool(name="w_load", bufs=PASSES))
         w_stage = pools.enter_context(tc.tile_pool(name="w_stage", bufs=2))
         gi_pool = pools.enter_context(tc.tile_pool(name="gi", bufs=3))
         work = pools.enter_context(tc.tile_pool(name="work", bufs=3))
@@ -41,19 +42,25 @@ def tile_grucellmodel_pa_v_kernel(tc, input_seq, W_ih, b_ih, gh, gi, grad_out, o
         psum_x = pools.enter_context(tc.psum_pool(name="psum_x", bufs=3))
         psum_an = pools.enter_context(tc.psum_pool(name="psum_an", bufs=2))
 
+        w_view = W_ih.rearrange("(g j p) n -> g p j n", j=PACK, p=P)
+        w_raws = []
+        for g in range(PASSES):
+            w_raw = w_load.tile([P, PACK, I], BF16, name="w_raw")
+            nc.sync.dma_start(out=w_raw[:], in_=w_view[g])
+            w_raws.append(w_raw)
         gh_sb = const.tile([P, GATES * H], BF16)
         nc.sync.dma_start(out=gh_sb[:], in_=gh)
         gi_tiles = {}
 
-        def load_gi(t):
+        go_sb = const.tile([P, T, H], BF16)
+
+        def load_step(t):
             gi_t = gi_pool.tile([P, GATES * H], F32, name="gi_t")
             nc.sync.dma_start(out=gi_t[:], in_=gi[t])
             gi_tiles[t] = gi_t
+            nc.sync.dma_start(out=go_sb[:, t, :], in_=grad_out[:, t, :])
 
-        load_gi(0)
-        go_sb = const.tile([P, T, H], BF16)
-        GO_CHUNK = 4
-        nc.sync.dma_start(out=go_sb[:, 0:GO_CHUNK, :], in_=grad_out[:, 0:GO_CHUNK, :])
+        load_step(0)
 
         ident_f32 = const.tile([P, P], F32)
         make_identity(nc, ident_f32[:])
@@ -68,22 +75,26 @@ def tile_grucellmodel_pa_v_kernel(tc, input_seq, W_ih, b_ih, gh, gi, grad_out, o
         nc.vector.tensor_scalar(
             out=neg_hn[:], in0=gh_sb[:, 2 * H : 3 * H], scalar1=-1.0, scalar2=None, op0=ALU.mult
         )
-        neg_hn_t = psum_fixed.tile([P, BLOCKS, B], BF16)
-        for blk in range(BLOCKS):
-            nc.tensor.transpose(neg_hn_t[:, blk, :], neg_hn[:, blk * P : (blk + 1) * P], ident_bf16[:])
+        def transpose_bf16(dst, src):
+            for half in range(HALVES):
+                for j in range(PACK):
+                    blk = half * PACK + j
+                    nc.tensor.transpose(
+                        dst[:, j, half * B : (half + 1) * B], src[:, blk * P : (blk + 1) * P], ident_bf16[:]
+                    )
+
+        neg_hn_t = psum_fixed.tile([P, PACK, HALVES * B], BF16)
+        transpose_bf16(neg_hn_t, neg_hn)
 
         w_codes = const.tile([P, PASSES, I], U32, align_bytes=64)
         w_scales = const.tile([P, PASSES, I], U8, align_bytes=64)
-        w_view = W_ih.rearrange("(g j p) n -> g p j n", j=PACK, p=P)
         w_grouped = {}
 
         def group_w(g):
-            w_raw = w_stage.tile([P, PACK, I], BF16, name="w_raw")
-            nc.sync.dma_start(out=w_raw[:], in_=w_view[g])
             w_grp = w_stage.tile([P, I, PACK], BF16, name="w_grp", align_bytes=64)
             nc.vector.tensor_copy(
                 out=w_grp[:].rearrange("p (c i) j -> p c j i", i=4),
-                in_=w_raw[:].rearrange("p j (c i) -> p c j i", i=4),
+                in_=w_raws[g][:].rearrange("p j (c i) -> p c j i", i=4),
             )
             w_grouped[g] = w_grp
 
@@ -104,6 +115,9 @@ def tile_grucellmodel_pa_v_kernel(tc, input_seq, W_ih, b_ih, gh, gi, grad_out, o
 
         def by_token(flat, half):
             return flat[:, half * K_PASS : (half + 1) * K_PASS].rearrange("p (b j) -> p b j", j=PACK)
+
+        def all_tokens(flat):
+            return flat[:].rearrange("p (c j) -> p c j", j=PACK)
 
         def gates_r_z(t):
             gi_t = gi_tiles[t]
@@ -139,33 +153,29 @@ def tile_grucellmodel_pa_v_kernel(tc, input_seq, W_ih, b_ih, gh, gi, grad_out, o
                     cols = slice(2 * H + half * K_PASS + j * P, 2 * H + half * K_PASS + (j + 1) * P)
                     nc.tensor.transpose(a_half[:, j, :], gi_t[:, cols], ident_f32[:])
                 a_n.append(a_half)
-            dh_t = psum_fixed.tile([P, BLOCKS, B], BF16, name="dh_t")
-            for blk in range(BLOCKS):
-                nc.tensor.transpose(dh_t[:, blk, :], go_sb[:, t, blk * P : (blk + 1) * P], ident_bf16[:])
+            dh_t = psum_fixed.tile([P, PACK, HALVES * B], BF16, name="dh_t")
+            transpose_bf16(dh_t, go_sb[:, t, :])
 
             n = work.tile([P, H], F32, name="n")
-            nc.vector.tensor_tensor(
-                out=n[:].rearrange("p (h b j) -> p h b j", h=HALVES, j=PACK),
-                in0=tiles["r"][:].rearrange("p (h b j) -> p h b j", h=HALVES, j=PACK),
-                in1=neg_hn_t[:].rearrange("p (h j) b -> p h b j", h=HALVES),
-                op=ALU.mult,
-            )
-            q = work.tile([P, H], F32, name="q")
+            for half in range(HALVES):
+                nc.vector.tensor_tensor(
+                    out=by_token(n, half), in0=by_token(tiles["r"], half),
+                    in1=neg_hn_t[:, :, half * B : (half + 1) * B].rearrange("p j b -> p b j"), op=ALU.mult,
+                )
             for half in range(HALVES):
                 nc.vector.tensor_tensor(
                     out=by_token(n, half), in0=a_n[half][:].rearrange("p j b -> p b j"),
                     in1=by_token(n, half), op=ALU.subtract,
                 )
-            for half in range(HALVES):
-                blocks = slice(half * PACK, (half + 1) * PACK)
-                nc.vector.scalar_tensor_tensor(
-                    out=by_token(q, half), in0=by_token(tiles["z"], half), scalar=1.0,
-                    in1=dh_t[:, blocks, :].rearrange("p j b -> p b j"), op0=ALU.subtract, op1=ALU.mult,
-                )
-                nc.vector.scalar_tensor_tensor(
-                    out=by_token(tiles["sr"], half), in0=by_token(tiles["sr"], half), scalar=0.25,
-                    in1=neg_hn_t[:, blocks, :].rearrange("p j b -> p b j"), op0=ALU.subtract, op1=ALU.mult,
-                )
+            q = work.tile([P, H], F32, name="q")
+            nc.vector.scalar_tensor_tensor(
+                out=all_tokens(q), in0=all_tokens(tiles["z"]), scalar=1.0,
+                in1=dh_t[:].rearrange("p j c -> p c j"), op0=ALU.subtract, op1=ALU.mult,
+            )
+            nc.vector.scalar_tensor_tensor(
+                out=all_tokens(tiles["sr"]), in0=all_tokens(tiles["sr"]), scalar=0.25,
+                in1=neg_hn_t[:].rearrange("p j c -> p c j"), op0=ALU.subtract, op1=ALU.mult,
+            )
             nc.scalar.activation(out=n[:], in_=n[:], func=FUNC.Tanh)
             sn = work.tile([P, H], F32, name="sn")
             nc.scalar.activation(out=sn[:], in_=n[:], func=FUNC.Square)
@@ -176,21 +186,22 @@ def tile_grucellmodel_pa_v_kernel(tc, input_seq, W_ih, b_ih, gh, gi, grad_out, o
         def gradients(t):
             tiles = live[t]
             dgi = quant.tile([P, GATES, H], BF16, name="dgi", align_bytes=64)
+            nc.vector.tensor_tensor(out=tiles["n"][:], in0=tiles["n"][:], in1=tiles["z"][:], op=ALU.mult)
             nc.vector.scalar_tensor_tensor(
                 out=tiles["sn"][:], in0=tiles["sn"][:], scalar=1.0, in1=tiles["q"][:],
                 op0=ALU.subtract, op1=ALU.mult,
             )
-            nc.vector.tensor_tensor(out=tiles["n"][:], in0=tiles["n"][:], in1=tiles["z"][:], op=ALU.mult)
             nc.scalar.copy(out=dgi[:, 2, :], in_=tiles["sn"][:])
-            nc.gpsimd.tensor_tensor(out=dgi[:, 1, :], in0=tiles["n"][:], in1=tiles["q"][:], op=ALU.mult)
-            nc.gpsimd.tensor_tensor(out=dgi[:, 0, :], in0=tiles["sr"][:], in1=tiles["sn"][:], op=ALU.mult)
+            engine = nc.gpsimd if t < T - 1 else nc.vector
+            engine.tensor_tensor(out=dgi[:, 1, :], in0=tiles["n"][:], in1=tiles["q"][:], op=ALU.mult)
+            engine.tensor_tensor(out=dgi[:, 0, :], in0=tiles["sr"][:], in1=tiles["sn"][:], op=ALU.mult)
             tiles["dgi"] = dgi
 
         def quantise(t):
             tiles = live[t]
             codes = quant.tile([P, GATES, H // PACK], U32, name="codes", align_bytes=64)
             scales = quant.tile([P, GATES, H // PACK], U8, name="scales", align_bytes=64)
-            for gate in (2, 1, 0):
+            for gate in GATE_ORDER:
                 nc.vector.quantize_mx(
                     out=codes[:, gate, :].bitcast(E5M2X4), scales=scales[:, gate, :], in_=tiles["dgi"][:, gate, :]
                 )
@@ -200,7 +211,8 @@ def tile_grucellmodel_pa_v_kernel(tc, input_seq, W_ih, b_ih, gh, gi, grad_out, o
         def multiply(t):
             tiles = live[t]
             acc = psum_fixed.tile([B, I], F32, name="acc")
-            for g in range(PASSES):
+            pass_order = [gate * HALVES + half for gate in GATE_ORDER for half in range(HALVES)]
+            for g in pass_order:
                 gate, half = divmod(g, HALVES)
                 tokens = slice(half * B, (half + 1) * B)
                 nc.tensor.matmul_mx(
@@ -209,8 +221,8 @@ def tile_grucellmodel_pa_v_kernel(tc, input_seq, W_ih, b_ih, gh, gi, grad_out, o
                     lhsT_scale=tiles["scales"][:, gate, tokens],
                     rhs=w_codes[:, g, :].bitcast(E4M3X4),
                     rhs_scale=w_scales[:, g, :],
-                    start=(g == 0),
-                    stop=(g == PASSES - 1),
+                    start=(g == pass_order[0]),
+                    stop=(g == pass_order[-1]),
                 )
             o_sb = result.tile([B, I], F32, name="o_sb")
             nc.scalar.copy(out=o_sb[:], in_=acc[:])
@@ -218,15 +230,15 @@ def tile_grucellmodel_pa_v_kernel(tc, input_seq, W_ih, b_ih, gh, gi, grad_out, o
 
         STAGES = ((gradients, 2), (gate_n, 1), (quantise, 3), (multiply, 3), (gates_r_z, 0))
         with tc.manual_schedule(engines={mybir.EngineType.DVE, mybir.EngineType.Pool}):
-            for step in range(T + 3):
+            for step in range(T + 1):
                 ahead = step + 1
                 if ahead < T:
-                    load_gi(ahead)
-                    if ahead % GO_CHUNK == 0:
-                        nc.sync.dma_start(
-                            out=go_sb[:, ahead : ahead + GO_CHUNK, :], in_=grad_out[:, ahead : ahead + GO_CHUNK, :]
-                        )
+                    load_step(ahead)
                 for stage, lag in STAGES:
                     t = step - lag
                     if 0 <= t < T:
                         stage(t)
+            for stage, t in (
+                (quantise, T - 2), (multiply, T - 2), (gradients, T - 1), (quantise, T - 1), (multiply, T - 1)
+            ):
+                stage(t)

@@ -61,6 +61,7 @@ def tile_grucellmodel_pa_v_kernel(tc, input_seq, W_ih, b_ih, gh, gi, grad_out, o
             nc.sync.dma_start(out=go_sb[:, t, :], in_=grad_out[:, t, :])
 
         load_step(0)
+        load_step(1)
 
         ident_f32 = const.tile([P, P], F32)
         make_identity(nc, ident_f32[:])
@@ -119,43 +120,55 @@ def tile_grucellmodel_pa_v_kernel(tc, input_seq, W_ih, b_ih, gh, gi, grad_out, o
         def all_tokens(flat):
             return flat[:].rearrange("p (c j) -> p c j", j=PACK)
 
-        def gates_r_z(t):
-            gi_t = gi_tiles[t]
-            r = work.tile([P, H], F32, name="r")
-            z = work.tile([P, H], F32, name="z")
-            for gate, dst in ((0, r), (1, z)):
-                for half in range(HALVES):
-                    x = psum_x.tile([P, PACK, B], F32, name="x")
-                    for j in range(PACK):
-                        cols = slice(gate * H + half * K_PASS + j * P, gate * H + half * K_PASS + (j + 1) * P)
-                        nc.tensor.matmul(
-                            x[:, j, :], lhsT=gi_t[:, cols], rhs=ident_f32[:],
-                            is_transpose=True, start=True, stop=False,
-                        )
-                        nc.tensor.matmul(
-                            x[:, j, :], lhsT=g_rz[:, cols], rhs=ident_f32[:],
-                            is_transpose=True, start=False, stop=True,
-                        )
-                    nc.scalar.activation(
-                        out=by_token(dst, half), in_=x[:].rearrange("p j b -> p b j"), func=FUNC.Sigmoid
-                    )
-            sr = work.tile([P, H], F32, name="sr")
-            nc.scalar.activation(out=sr[:], in_=r[:], func=FUNC.Square, bias=minus_half[:], scale=1.0)
-            live[t] = {"r": r, "z": z, "sr": sr}
+        def transpose_gate(t, gate, half):
+            x = psum_x.tile([P, PACK, B], F32, name="x")
+            for j in range(PACK):
+                cols = slice(gate * H + half * K_PASS + j * P, gate * H + half * K_PASS + (j + 1) * P)
+                nc.tensor.matmul(
+                    x[:, j, :], lhsT=gi_tiles[t][:, cols], rhs=ident_f32[:],
+                    is_transpose=True, start=True, stop=False,
+                )
+                nc.tensor.matmul(
+                    x[:, j, :], lhsT=g_rz[:, cols], rhs=ident_f32[:],
+                    is_transpose=True, start=False, stop=True,
+                )
+            live.setdefault(t, {})[("x", gate, half)] = x
 
-        def gate_n(t):
-            gi_t = gi_tiles[t]
+        def sigmoid(t, gate, half):
             tiles = live[t]
+            name = ("r", "z")[gate]
+            if half == 0:
+                if gate == 0:
+                    r = work.tile([P, H], F32, name="r")
+                    tiles["r"] = r
+                else:
+                    z = work.tile([P, H], F32, name="z")
+                    tiles["z"] = z
+            nc.scalar.activation(
+                out=by_token(tiles[name], half), in_=tiles[("x", gate, half)][:].rearrange("p j b -> p b j"),
+                func=FUNC.Sigmoid,
+            )
+
+        def square_r(t):
+            sr = work.tile([P, H], F32, name="sr")
+            nc.scalar.activation(out=sr[:], in_=live[t]["r"][:], func=FUNC.Square, bias=minus_half[:], scale=1.0)
+            live[t]["sr"] = sr
+
+        def transpose_n(t):
             a_n = []
             for half in range(HALVES):
                 a_half = psum_an.tile([P, PACK, B], F32, name="a_half")
                 for j in range(PACK):
                     cols = slice(2 * H + half * K_PASS + j * P, 2 * H + half * K_PASS + (j + 1) * P)
-                    nc.tensor.transpose(a_half[:, j, :], gi_t[:, cols], ident_f32[:])
+                    nc.tensor.transpose(a_half[:, j, :], gi_tiles[t][:, cols], ident_f32[:])
                 a_n.append(a_half)
             dh_t = psum_fixed.tile([P, PACK, HALVES * B], BF16, name="dh_t")
             transpose_bf16(dh_t, go_sb[:, t, :])
+            live[t]["a_n"] = a_n
+            live[t]["dh_t"] = dh_t
 
+        def gate_n(t):
+            tiles = live[t]
             n = work.tile([P, H], F32, name="n")
             for half in range(HALVES):
                 nc.vector.tensor_tensor(
@@ -164,21 +177,21 @@ def tile_grucellmodel_pa_v_kernel(tc, input_seq, W_ih, b_ih, gh, gi, grad_out, o
                 )
             for half in range(HALVES):
                 nc.vector.tensor_tensor(
-                    out=by_token(n, half), in0=a_n[half][:].rearrange("p j b -> p b j"),
+                    out=by_token(n, half), in0=tiles["a_n"][half][:].rearrange("p j b -> p b j"),
                     in1=by_token(n, half), op=ALU.subtract,
                 )
+            nc.scalar.activation(out=n[:], in_=n[:], func=FUNC.Tanh)
+            sn = work.tile([P, H], F32, name="sn")
+            nc.scalar.activation(out=sn[:], in_=n[:], func=FUNC.Square)
             q = work.tile([P, H], F32, name="q")
             nc.vector.scalar_tensor_tensor(
                 out=all_tokens(q), in0=all_tokens(tiles["z"]), scalar=1.0,
-                in1=dh_t[:].rearrange("p j c -> p c j"), op0=ALU.subtract, op1=ALU.mult,
+                in1=tiles["dh_t"][:].rearrange("p j c -> p c j"), op0=ALU.subtract, op1=ALU.mult,
             )
             nc.vector.scalar_tensor_tensor(
                 out=all_tokens(tiles["sr"]), in0=all_tokens(tiles["sr"]), scalar=0.25,
                 in1=neg_hn_t[:].rearrange("p j c -> p c j"), op0=ALU.subtract, op1=ALU.mult,
             )
-            nc.scalar.activation(out=n[:], in_=n[:], func=FUNC.Tanh)
-            sn = work.tile([P, H], F32, name="sn")
-            nc.scalar.activation(out=sn[:], in_=n[:], func=FUNC.Square)
             tiles["n"] = n
             tiles["q"] = q
             tiles["sn"] = sn
@@ -191,10 +204,10 @@ def tile_grucellmodel_pa_v_kernel(tc, input_seq, W_ih, b_ih, gh, gi, grad_out, o
                 out=tiles["sn"][:], in0=tiles["sn"][:], scalar=1.0, in1=tiles["q"][:],
                 op0=ALU.subtract, op1=ALU.mult,
             )
-            nc.scalar.copy(out=dgi[:, 2, :], in_=tiles["sn"][:])
             engine = nc.gpsimd if t < T - 1 else nc.vector
             engine.tensor_tensor(out=dgi[:, 1, :], in0=tiles["n"][:], in1=tiles["q"][:], op=ALU.mult)
             engine.tensor_tensor(out=dgi[:, 0, :], in0=tiles["sr"][:], in1=tiles["sn"][:], op=ALU.mult)
+            nc.scalar.copy(out=dgi[:, 2, :], in_=tiles["sn"][:])
             tiles["dgi"] = dgi
 
         def quantise(t):
@@ -224,21 +237,42 @@ def tile_grucellmodel_pa_v_kernel(tc, input_seq, W_ih, b_ih, gh, gi, grad_out, o
                     start=(g == pass_order[0]),
                     stop=(g == pass_order[-1]),
                 )
+            tiles["acc"] = acc
+
+        def store(t):
             o_sb = result.tile([B, I], F32, name="o_sb")
-            nc.scalar.copy(out=o_sb[:], in_=acc[:])
+            nc.scalar.copy(out=o_sb[:], in_=live[t]["acc"][:])
             nc.sync.dma_start(out=out[t], in_=o_sb[:])
 
-        STAGES = ((gradients, 2), (gate_n, 1), (quantise, 3), (multiply, 3), (gates_r_z, 0))
-        with tc.manual_schedule(engines={mybir.EngineType.DVE, mybir.EngineType.Pool}):
-            for step in range(T + 1):
-                ahead = step + 1
-                if ahead < T:
-                    load_step(ahead)
-                for stage, lag in STAGES:
-                    t = step - lag
-                    if 0 <= t < T:
-                        stage(t)
-            for stage, t in (
-                (quantise, T - 2), (multiply, T - 2), (gradients, T - 1), (quantise, T - 1), (multiply, T - 1)
-            ):
-                stage(t)
+        def in_range(t):
+            return 0 <= t < T
+
+        with tc.manual_schedule():
+            for step in range(T + 6):
+                if in_range(step - 1):
+                    transpose_gate(step - 1, 1, 1)
+                    sigmoid(step - 1, 1, 1)
+                if in_range(step + 2):
+                    load_step(step + 2)
+                if in_range(step):
+                    transpose_gate(step, 0, 0)
+                    transpose_gate(step, 0, 1)
+                    transpose_gate(step, 1, 0)
+                if in_range(step - 5):
+                    store(step - 5)
+                if in_range(step - 4):
+                    multiply(step - 4)
+                if step - 2 == T - 1:
+                    quantise(step - 3)
+                if in_range(step - 2):
+                    gradients(step - 2)
+                if in_range(step - 1):
+                    gate_n(step - 1)
+                if in_range(step):
+                    transpose_n(step)
+                    sigmoid(step, 0, 0)
+                    sigmoid(step, 0, 1)
+                    square_r(step)
+                    sigmoid(step, 1, 0)
+                if in_range(step - 3) and step - 2 != T - 1:
+                    quantise(step - 3)

@@ -214,9 +214,11 @@ def tile_grucellmodel_pa_v_kernel(tc, input_seq, W_ih, b_ih, gh, gi, grad_out, o
             tiles = live[t]
             codes = quant.tile([P, GATES, H // PACK], U32, name="codes", align_bytes=64)
             scales = quant.tile([P, GATES, H // PACK], U8, name="scales", align_bytes=64)
-            for gate in GATE_ORDER:
+            for gates in (slice(1, 3), slice(0, 1)):
                 nc.vector.quantize_mx(
-                    out=codes[:, gate, :].bitcast(E5M2X4), scales=scales[:, gate, :], in_=tiles["dgi"][:, gate, :]
+                    out=codes[:, gates, :].rearrange("p g c -> p (g c)").bitcast(E5M2X4),
+                    scales=scales[:, gates, :].rearrange("p g c -> p (g c)"),
+                    in_=tiles["dgi"][:, gates, :].rearrange("p g c -> p (g c)"),
                 )
             tiles["codes"] = codes
             tiles["scales"] = scales
@@ -248,7 +250,7 @@ def tile_grucellmodel_pa_v_kernel(tc, input_seq, W_ih, b_ih, gh, gi, grad_out, o
             return 0 <= t < T
 
         with tc.manual_schedule():
-            for step in range(T + 6):
+            for step in range(T + 1):
                 if in_range(step - 1):
                     transpose_gate(step - 1, 1, 1)
                     sigmoid(step - 1, 1, 1)
@@ -262,8 +264,6 @@ def tile_grucellmodel_pa_v_kernel(tc, input_seq, W_ih, b_ih, gh, gi, grad_out, o
                     store(step - 5)
                 if in_range(step - 4):
                     multiply(step - 4)
-                if step - 2 == T - 1:
-                    quantise(step - 3)
                 if in_range(step - 2):
                     gradients(step - 2)
                 if in_range(step - 1):
@@ -274,5 +274,15 @@ def tile_grucellmodel_pa_v_kernel(tc, input_seq, W_ih, b_ih, gh, gi, grad_out, o
                     sigmoid(step, 0, 1)
                     square_r(step)
                     sigmoid(step, 1, 0)
-                if in_range(step - 3) and step - 2 != T - 1:
+                if in_range(step - 3):
                     quantise(step - 3)
+            store(T - 4)
+            multiply(T - 3)
+            store(T - 3)
+            quantise(T - 2)
+            multiply(T - 2)
+            gradients(T - 1)
+            store(T - 2)
+            quantise(T - 1)
+            multiply(T - 1)
+            store(T - 1)

@@ -22,6 +22,7 @@ K_PASS = P * PACK
 HALVES = H // K_PASS
 GATES = 3
 PASSES = GATES * HALVES
+EARLY_PASSES = 3
 GATE_ORDER = (1, 2, 0)
 
 FLOPS = 2 * T * B * GATES * H * I
@@ -33,7 +34,7 @@ def tile_grucellmodel_pa_v_kernel(tc, input_seq, W_ih, b_ih, gh, gi, grad_out, o
     with ExitStack() as pools:
         const = pools.enter_context(tc.tile_pool(name="const", bufs=1))
         w_load = pools.enter_context(tc.tile_pool(name="w_load", bufs=PASSES))
-        w_stage = pools.enter_context(tc.tile_pool(name="w_stage", bufs=2))
+        w_stage = pools.enter_context(tc.tile_pool(name="w_stage", bufs=3))
         gi_pool = pools.enter_context(tc.tile_pool(name="gi", bufs=3))
         work = pools.enter_context(tc.tile_pool(name="work", bufs=3))
         quant = pools.enter_context(tc.tile_pool(name="quant", bufs=2))
@@ -44,10 +45,14 @@ def tile_grucellmodel_pa_v_kernel(tc, input_seq, W_ih, b_ih, gh, gi, grad_out, o
 
         w_view = W_ih.rearrange("(g j p) n -> g p j n", j=PACK, p=P)
         w_raws = []
-        for g in range(PASSES):
+
+        def load_w(g):
             w_raw = w_load.tile([P, PACK, I], BF16, name="w_raw")
             nc.sync.dma_start(out=w_raw[:], in_=w_view[g])
             w_raws.append(w_raw)
+
+        for g in range(EARLY_PASSES):
+            load_w(g)
         gh_sb = const.tile([P, GATES * H], BF16)
         nc.sync.dma_start(out=gh_sb[:], in_=gh)
         gi_tiles = {}
@@ -61,6 +66,8 @@ def tile_grucellmodel_pa_v_kernel(tc, input_seq, W_ih, b_ih, gh, gi, grad_out, o
             nc.sync.dma_start(out=go_sb[:, t, :], in_=grad_out[:, t, :])
 
         load_step(0)
+        for g in range(EARLY_PASSES, PASSES):
+            load_w(g)
         load_step(1)
 
         ident_f32 = const.tile([P, P], F32)
@@ -93,10 +100,16 @@ def tile_grucellmodel_pa_v_kernel(tc, input_seq, W_ih, b_ih, gh, gi, grad_out, o
 
         def group_w(g):
             w_grp = w_stage.tile([P, I, PACK], BF16, name="w_grp", align_bytes=64)
-            nc.vector.tensor_copy(
-                out=w_grp[:].rearrange("p (c i) j -> p c j i", i=4),
-                in_=w_raws[g][:].rearrange("p j (c i) -> p c j i", i=4),
-            )
+            if g < EARLY_PASSES:
+                nc.vector.tensor_copy(
+                    out=w_grp[:].rearrange("p (c i) j -> p c j i", i=4),
+                    in_=w_raws[g][:].rearrange("p j (c i) -> p c j i", i=4),
+                )
+            else:
+                nc.gpsimd.tensor_scalar(
+                    out=w_grp[:], in0=w_raws[g][:].rearrange("p j n -> p n j"),
+                    scalar1=1.0, scalar2=0.0, op0=ALU.mult, op1=ALU.add,
+                )
             w_grouped[g] = w_grp
 
         def quantise_w(g):
@@ -107,10 +120,12 @@ def tile_grucellmodel_pa_v_kernel(tc, input_seq, W_ih, b_ih, gh, gi, grad_out, o
             )
 
         group_w(0)
-        for g in range(1, PASSES):
+        for g in range(1, EARLY_PASSES):
             group_w(g)
             quantise_w(g - 1)
-        quantise_w(PASSES - 1)
+        quantise_w(EARLY_PASSES - 1)
+        for g in range(EARLY_PASSES, PASSES):
+            group_w(g)
 
         live = {}
 
@@ -274,6 +289,9 @@ def tile_grucellmodel_pa_v_kernel(tc, input_seq, W_ih, b_ih, gh, gi, grad_out, o
                     sigmoid(step, 0, 1)
                     square_r(step)
                     sigmoid(step, 1, 0)
+                if step == 2:
+                    for g in range(EARLY_PASSES, PASSES):
+                        quantise_w(g)
                 if in_range(step - 3):
                     quantise(step - 3)
             store(T - 4)

@@ -23,6 +23,7 @@ HALVES = H // K_PASS
 GATES = 3
 PASSES = GATES * HALVES
 EARLY_PASSES = 3
+VECTOR_DZ = 256
 GATE_ORDER = (1, 2, 0)
 
 FLOPS = 2 * T * B * GATES * H * I
@@ -219,9 +220,16 @@ def tile_grucellmodel_pa_v_kernel(tc, input_seq, W_ih, b_ih, gh, gi, grad_out, o
                 out=tiles["sn"][:], in0=tiles["sn"][:], scalar=1.0, in1=tiles["q"][:],
                 op0=ALU.subtract, op1=ALU.mult,
             )
+            split = VECTOR_DZ if t < T - 1 else H
             engine = nc.gpsimd if t < T - 1 else nc.vector
-            engine.tensor_tensor(out=dgi[:, 1, :], in0=tiles["n"][:], in1=tiles["q"][:], op=ALU.mult)
+            nc.vector.tensor_tensor(
+                out=dgi[:, 1, :split], in0=tiles["n"][:, :split], in1=tiles["q"][:, :split], op=ALU.mult
+            )
             engine.tensor_tensor(out=dgi[:, 0, :], in0=tiles["sr"][:], in1=tiles["sn"][:], op=ALU.mult)
+            if split < H:
+                engine.tensor_tensor(
+                    out=dgi[:, 1, split:], in0=tiles["n"][:, split:], in1=tiles["q"][:, split:], op=ALU.mult
+                )
             nc.scalar.copy(out=dgi[:, 2, :], in_=tiles["sn"][:])
             tiles["dgi"] = dgi
 

@@ -23,7 +23,8 @@ HALVES = H // K_PASS
 GATES = 3
 PASSES = GATES * HALVES
 EARLY_PASSES = 3
-VECTOR_DZ = 256
+VECTOR_DZ = 128
+GPSIMD_GROUPS = (3, 4)
 GATE_ORDER = (1, 2, 0)
 
 FLOPS = 2 * T * B * GATES * H * I
@@ -52,24 +53,44 @@ def tile_grucellmodel_pa_v_kernel(tc, input_seq, W_ih, b_ih, gh, gi, grad_out, o
             nc.sync.dma_start(out=w_raw[:], in_=w_view[g])
             w_raws.append(w_raw)
 
-        for g in range(EARLY_PASSES):
-            load_w(g)
         gh_sb = const.tile([P, GATES * H], BF16)
-        nc.sync.dma_start(out=gh_sb[:], in_=gh)
+
+        def load_gh(gates):
+            cols = slice(gates.start * H, gates.stop * H)
+            nc.sync.dma_start(out=gh_sb[:, cols], in_=gh[:, cols])
+
         gi_tiles = {}
 
         go_sb = const.tile([P, T, H], BF16)
 
-        def load_step(t):
-            gi_t = gi_pool.tile([P, GATES * H], F32, name="gi_t")
-            nc.sync.dma_start(out=gi_t[:], in_=gi[t])
-            gi_tiles[t] = gi_t
+        def load_gates(t, gates):
+            if t not in gi_tiles:
+                gi_t = gi_pool.tile([P, GATES * H], F32, name="gi_t")
+                gi_tiles[t] = gi_t
+            cols = slice(gates.start * H, gates.stop * H)
+            nc.sync.dma_start(out=gi_tiles[t][:, cols], in_=gi[t][:, cols])
+
+        def load_go(t):
             nc.sync.dma_start(out=go_sb[:, t, :], in_=grad_out[:, t, :])
 
-        load_step(0)
-        for g in range(EARLY_PASSES, PASSES):
+        def load_step(t):
+            load_gates(t, slice(0, GATES))
+            load_go(t)
+
+        for g in range(EARLY_PASSES):
             load_w(g)
-        load_step(1)
+        load_gh(slice(0, 1))
+        load_gates(0, slice(0, 1))
+        load_gh(slice(1, 3))
+        load_gates(0, slice(2, 3))
+        load_gates(0, slice(1, 2))
+        load_go(0)
+        load_w(3)
+        load_gates(1, slice(0, 1))
+        load_w(4)
+        load_gates(1, slice(1, 3))
+        load_go(1)
+        load_w(5)
 
         ident_f32 = const.tile([P, P], F32)
         make_identity(nc, ident_f32[:])
@@ -79,11 +100,8 @@ def tile_grucellmodel_pa_v_kernel(tc, input_seq, W_ih, b_ih, gh, gi, grad_out, o
         nc.vector.memset(minus_half[:], -0.5)
 
         g_rz = const.tile([P, 2 * H], F32)
-        nc.vector.tensor_copy(out=g_rz[:], in_=gh_sb[:, 0 : 2 * H])
         neg_hn = const.tile([P, H], BF16)
-        nc.vector.tensor_scalar(
-            out=neg_hn[:], in0=gh_sb[:, 2 * H : 3 * H], scalar1=-1.0, scalar2=None, op0=ALU.mult
-        )
+
         def transpose_bf16(dst, src):
             for half in range(HALVES):
                 for j in range(PACK):
@@ -93,7 +111,6 @@ def tile_grucellmodel_pa_v_kernel(tc, input_seq, W_ih, b_ih, gh, gi, grad_out, o
                     )
 
         neg_hn_t = psum_fixed.tile([P, PACK, HALVES * B], BF16)
-        transpose_bf16(neg_hn_t, neg_hn)
 
         w_codes = const.tile([P, PASSES, I], U32, align_bytes=64)
         w_scales = const.tile([P, PASSES, I], U8, align_bytes=64)
@@ -101,15 +118,15 @@ def tile_grucellmodel_pa_v_kernel(tc, input_seq, W_ih, b_ih, gh, gi, grad_out, o
 
         def group_w(g):
             w_grp = w_stage.tile([P, I, PACK], BF16, name="w_grp", align_bytes=64)
-            if g < EARLY_PASSES:
-                nc.vector.tensor_copy(
-                    out=w_grp[:].rearrange("p (c i) j -> p c j i", i=4),
-                    in_=w_raws[g][:].rearrange("p j (c i) -> p c j i", i=4),
-                )
-            else:
+            if g in GPSIMD_GROUPS:
                 nc.gpsimd.tensor_scalar(
                     out=w_grp[:], in0=w_raws[g][:].rearrange("p j n -> p n j"),
                     scalar1=1.0, scalar2=0.0, op0=ALU.mult, op1=ALU.add,
+                )
+            else:
+                nc.vector.tensor_copy(
+                    out=w_grp[:].rearrange("p (c i) j -> p c j i", i=4),
+                    in_=w_raws[g][:].rearrange("p j (c i) -> p c j i", i=4),
                 )
             w_grouped[g] = w_grp
 
@@ -121,12 +138,16 @@ def tile_grucellmodel_pa_v_kernel(tc, input_seq, W_ih, b_ih, gh, gi, grad_out, o
             )
 
         group_w(0)
-        for g in range(1, EARLY_PASSES):
-            group_w(g)
-            quantise_w(g - 1)
-        quantise_w(EARLY_PASSES - 1)
-        for g in range(EARLY_PASSES, PASSES):
-            group_w(g)
+        group_w(1)
+        quantise_w(0)
+        nc.vector.tensor_copy(out=g_rz[:, 0:H], in_=gh_sb[:, 0:H])
+        group_w(2)
+        quantise_w(1)
+        nc.vector.tensor_scalar(
+            out=neg_hn[:], in0=gh_sb[:, 2 * H : 3 * H], scalar1=-1.0, scalar2=None, op0=ALU.mult
+        )
+        nc.vector.tensor_copy(out=g_rz[:, H:], in_=gh_sb[:, H : 2 * H])
+        quantise_w(2)
 
         live = {}
 
@@ -178,9 +199,11 @@ def tile_grucellmodel_pa_v_kernel(tc, input_seq, W_ih, b_ih, gh, gi, grad_out, o
                     cols = slice(2 * H + half * K_PASS + j * P, 2 * H + half * K_PASS + (j + 1) * P)
                     nc.tensor.transpose(a_half[:, j, :], gi_tiles[t][:, cols], ident_f32[:])
                 a_n.append(a_half)
+            live[t]["a_n"] = a_n
+
+        def transpose_dh(t):
             dh_t = psum_fixed.tile([P, PACK, HALVES * B], BF16, name="dh_t")
             transpose_bf16(dh_t, go_sb[:, t, :])
-            live[t]["a_n"] = a_n
             live[t]["dh_t"] = dh_t
 
         def gate_n(t):
@@ -199,62 +222,94 @@ def tile_grucellmodel_pa_v_kernel(tc, input_seq, W_ih, b_ih, gh, gi, grad_out, o
             nc.scalar.activation(out=n[:], in_=n[:], func=FUNC.Tanh)
             sn = work.tile([P, H], F32, name="sn")
             nc.scalar.activation(out=sn[:], in_=n[:], func=FUNC.Square)
-            q = work.tile([P, H], F32, name="q")
-            nc.vector.scalar_tensor_tensor(
-                out=all_tokens(q), in0=all_tokens(tiles["z"]), scalar=1.0,
-                in1=tiles["dh_t"][:].rearrange("p j c -> p c j"), op0=ALU.subtract, op1=ALU.mult,
-            )
-            nc.vector.scalar_tensor_tensor(
-                out=all_tokens(tiles["sr"]), in0=all_tokens(tiles["sr"]), scalar=0.25,
-                in1=neg_hn_t[:].rearrange("p j c -> p c j"), op0=ALU.subtract, op1=ALU.mult,
-            )
             tiles["n"] = n
-            tiles["q"] = q
+
+            def make_q():
+                q = work.tile([P, H], F32, name="q")
+                nc.vector.scalar_tensor_tensor(
+                    out=all_tokens(q), in0=all_tokens(tiles["z"]), scalar=1.0,
+                    in1=tiles["dh_t"][:].rearrange("p j c -> p c j"), op0=ALU.subtract, op1=ALU.mult,
+                )
+                tiles["q"] = q
+
+            def make_c():
+                nc.vector.scalar_tensor_tensor(
+                    out=all_tokens(tiles["sr"]), in0=all_tokens(tiles["sr"]), scalar=0.25,
+                    in1=neg_hn_t[:].rearrange("p j c -> p c j"), op0=ALU.subtract, op1=ALU.mult,
+                )
+
+            if t == 0:
+                make_c()
+                make_q()
+            else:
+                make_q()
+                make_c()
             tiles["sn"] = sn
+
+        def last_gradients(tiles, dgi):
+            nc.vector.scalar_tensor_tensor(
+                out=tiles["sn"][:], in0=tiles["sn"][:], scalar=1.0, in1=tiles["q"][:],
+                op0=ALU.subtract, op1=ALU.mult,
+            )
+            nc.scalar.copy(out=dgi[:, 2, :], in_=tiles["sn"][:])
+            nc.vector.tensor_tensor(out=tiles["n"][:], in0=tiles["n"][:], in1=tiles["z"][:], op=ALU.mult)
+            nc.vector.tensor_tensor(out=dgi[:, 1, :], in0=tiles["n"][:], in1=tiles["q"][:], op=ALU.mult)
+            quantise_gates(T - 1, slice(1, 3))
+            nc.vector.tensor_tensor(out=dgi[:, 0, :], in0=tiles["sr"][:], in1=tiles["sn"][:], op=ALU.mult)
+            quantise_gates(T - 1, slice(0, 1))
 
         def gradients(t):
             tiles = live[t]
-            dgi = quant.tile([P, GATES, H], BF16, name="dgi", align_bytes=64)
+            tiles["dgi"] = dgi = quant.tile([P, GATES, H], BF16, name="dgi", align_bytes=64)
+            if t == T - 1:
+                last_gradients(tiles, dgi)
+                return
             nc.vector.tensor_tensor(out=tiles["n"][:], in0=tiles["n"][:], in1=tiles["z"][:], op=ALU.mult)
             nc.vector.scalar_tensor_tensor(
                 out=tiles["sn"][:], in0=tiles["sn"][:], scalar=1.0, in1=tiles["q"][:],
                 op0=ALU.subtract, op1=ALU.mult,
             )
-            split = VECTOR_DZ if t < T - 1 else H
-            engine = nc.gpsimd if t < T - 1 else nc.vector
+            split = VECTOR_DZ
             nc.vector.tensor_tensor(
                 out=dgi[:, 1, :split], in0=tiles["n"][:, :split], in1=tiles["q"][:, :split], op=ALU.mult
             )
-            engine.tensor_tensor(out=dgi[:, 0, :], in0=tiles["sr"][:], in1=tiles["sn"][:], op=ALU.mult)
-            if split < H:
-                engine.tensor_tensor(
-                    out=dgi[:, 1, split:], in0=tiles["n"][:, split:], in1=tiles["q"][:, split:], op=ALU.mult
-                )
+            nc.gpsimd.tensor_tensor(out=dgi[:, 0, :], in0=tiles["sr"][:], in1=tiles["sn"][:], op=ALU.mult)
+            nc.gpsimd.tensor_tensor(
+                out=dgi[:, 1, split:], in0=tiles["n"][:, split:], in1=tiles["q"][:, split:], op=ALU.mult
+            )
             nc.scalar.copy(out=dgi[:, 2, :], in_=tiles["sn"][:])
-            tiles["dgi"] = dgi
+
+        def quantise_gates(t, gates):
+            tiles = live[t]
+            if "codes" not in tiles:
+                codes = quant.tile([P, GATES, H // PACK], U32, name="codes", align_bytes=64)
+                scales = quant.tile([P, GATES, H // PACK], U8, name="scales", align_bytes=64)
+                tiles["codes"] = codes
+                tiles["scales"] = scales
+            nc.vector.quantize_mx(
+                out=tiles["codes"][:, gates, :].rearrange("p g c -> p (g c)").bitcast(E5M2X4),
+                scales=tiles["scales"][:, gates, :].rearrange("p g c -> p (g c)"),
+                in_=tiles["dgi"][:, gates, :].rearrange("p g c -> p (g c)"),
+            )
 
         def quantise(t):
-            tiles = live[t]
-            codes = quant.tile([P, GATES, H // PACK], U32, name="codes", align_bytes=64)
-            scales = quant.tile([P, GATES, H // PACK], U8, name="scales", align_bytes=64)
-            for gates in (slice(1, 3), slice(0, 1)):
-                nc.vector.quantize_mx(
-                    out=codes[:, gates, :].rearrange("p g c -> p (g c)").bitcast(E5M2X4),
-                    scales=scales[:, gates, :].rearrange("p g c -> p (g c)"),
-                    in_=tiles["dgi"][:, gates, :].rearrange("p g c -> p (g c)"),
-                )
-            tiles["codes"] = codes
-            tiles["scales"] = scales
+            quantise_gates(t, slice(1, 3))
+            quantise_gates(t, slice(0, 1))
 
         def multiply(t):
             tiles = live[t]
-            acc = psum_fixed.tile([B, I], F32, name="acc")
+            if t == T - 1:
+                x = psum_x.tile([P, PACK, B], F32, name="x")
+                acc = x[:].rearrange("p j b -> p (j b)")
+            else:
+                acc_t = psum_fixed.tile([B, I], F32, name="acc")
+                acc = acc_t[:]
             pass_order = [gate * HALVES + half for gate in GATE_ORDER for half in range(HALVES)]
             for g in pass_order:
                 gate, half = divmod(g, HALVES)
                 tokens = slice(half * B, (half + 1) * B)
                 nc.tensor.matmul_mx(
-                    out=acc[:],
+                    out=acc,
                     lhsT=tiles["codes"][:, gate, tokens].bitcast(E5M2X4),
                     lhsT_scale=tiles["scales"][:, gate, tokens],
                     rhs=w_codes[:, g, :].bitcast(E4M3X4),
@@ -266,7 +321,7 @@ def tile_grucellmodel_pa_v_kernel(tc, input_seq, W_ih, b_ih, gh, gi, grad_out, o
 
         def store(t):
             o_sb = result.tile([B, I], F32, name="o_sb")
-            nc.scalar.copy(out=o_sb[:], in_=live[t]["acc"][:])
+            nc.scalar.copy(out=o_sb[:], in_=live[t]["acc"])
             nc.sync.dma_start(out=out[t], in_=o_sb[:])
 
         def in_range(t):
@@ -282,6 +337,9 @@ def tile_grucellmodel_pa_v_kernel(tc, input_seq, W_ih, b_ih, gh, gi, grad_out, o
                 if in_range(step):
                     transpose_gate(step, 0, 0)
                     transpose_gate(step, 0, 1)
+                    if step == 0:
+                        transpose_bf16(neg_hn_t, neg_hn)
+                        transpose_n(step)
                     transpose_gate(step, 1, 0)
                 if in_range(step - 5):
                     store(step - 5)
@@ -292,23 +350,31 @@ def tile_grucellmodel_pa_v_kernel(tc, input_seq, W_ih, b_ih, gh, gi, grad_out, o
                 if in_range(step - 1):
                     gate_n(step - 1)
                 if in_range(step):
-                    transpose_n(step)
+                    if step > 0:
+                        transpose_n(step)
+                    transpose_dh(step)
                     sigmoid(step, 0, 0)
                     sigmoid(step, 0, 1)
                     square_r(step)
                     sigmoid(step, 1, 0)
+                if step == 1:
+                    group_w(3)
+                    group_w(4)
                 if step == 2:
-                    for g in range(EARLY_PASSES, PASSES):
-                        quantise_w(g)
+                    group_w(5)
+                    quantise_w(3)
+                if step == 3:
+                    quantise_w(4)
                 if in_range(step - 3):
                     quantise(step - 3)
+                if step == 3:
+                    quantise_w(5)
             store(T - 4)
             multiply(T - 3)
             store(T - 3)
             quantise(T - 2)
             multiply(T - 2)
             gradients(T - 1)
-            store(T - 2)
-            quantise(T - 1)
             multiply(T - 1)
+            store(T - 2)
             store(T - 1)

@@ -23,7 +23,7 @@ HALVES = H // K_PASS
 GATES = 3
 PASSES = GATES * HALVES
 EARLY_PASSES = 3
-VECTOR_DZ = 128
+VECTOR_DZ = 256
 GPSIMD_GROUPS = (3, 4)
 GATE_ORDER = (1, 2, 0)
 
@@ -252,8 +252,8 @@ def tile_grucellmodel_pa_v_kernel(tc, input_seq, W_ih, b_ih, gh, gi, grad_out, o
                 op0=ALU.subtract, op1=ALU.mult,
             )
             nc.scalar.copy(out=dgi[:, 2, :], in_=tiles["sn"][:])
-            nc.vector.tensor_tensor(out=tiles["n"][:], in0=tiles["n"][:], in1=tiles["z"][:], op=ALU.mult)
-            nc.vector.tensor_tensor(out=dgi[:, 1, :], in0=tiles["n"][:], in1=tiles["q"][:], op=ALU.mult)
+            nc.vector.tensor_tensor(out=tiles["z"][:], in0=tiles["n"][:], in1=tiles["z"][:], op=ALU.mult)
+            nc.vector.tensor_tensor(out=dgi[:, 1, :], in0=tiles["z"][:], in1=tiles["q"][:], op=ALU.mult)
             quantise_gates(T - 1, slice(1, 3))
             nc.vector.tensor_tensor(out=dgi[:, 0, :], in0=tiles["sr"][:], in1=tiles["sn"][:], op=ALU.mult)
             quantise_gates(T - 1, slice(0, 1))
@@ -264,18 +264,18 @@ def tile_grucellmodel_pa_v_kernel(tc, input_seq, W_ih, b_ih, gh, gi, grad_out, o
             if t == T - 1:
                 last_gradients(tiles, dgi)
                 return
-            nc.vector.tensor_tensor(out=tiles["n"][:], in0=tiles["n"][:], in1=tiles["z"][:], op=ALU.mult)
+            nc.vector.tensor_tensor(out=tiles["z"][:], in0=tiles["n"][:], in1=tiles["z"][:], op=ALU.mult)
             nc.vector.scalar_tensor_tensor(
                 out=tiles["sn"][:], in0=tiles["sn"][:], scalar=1.0, in1=tiles["q"][:],
                 op0=ALU.subtract, op1=ALU.mult,
             )
             split = VECTOR_DZ
             nc.vector.tensor_tensor(
-                out=dgi[:, 1, :split], in0=tiles["n"][:, :split], in1=tiles["q"][:, :split], op=ALU.mult
+                out=dgi[:, 1, :split], in0=tiles["z"][:, :split], in1=tiles["q"][:, :split], op=ALU.mult
             )
             nc.gpsimd.tensor_tensor(out=dgi[:, 0, :], in0=tiles["sr"][:], in1=tiles["sn"][:], op=ALU.mult)
             nc.gpsimd.tensor_tensor(
-                out=dgi[:, 1, split:], in0=tiles["n"][:, split:], in1=tiles["q"][:, split:], op=ALU.mult
+                out=dgi[:, 1, split:], in0=tiles["z"][:, split:], in1=tiles["q"][:, split:], op=ALU.mult
             )
             nc.scalar.copy(out=dgi[:, 2, :], in_=tiles["sn"][:])
 

@@ -23,7 +23,7 @@ HALVES = H // K_PASS
 GATES = 3
 PASSES = GATES * HALVES
 EARLY_PASSES = 3
-VECTOR_DZ = 256
+VECTOR_DZ = 192
 GPSIMD_GROUPS = (3, 4)
 GATE_ORDER = (1, 2, 0)
 
@@ -220,8 +220,6 @@ def tile_grucellmodel_pa_v_kernel(tc, input_seq, W_ih, b_ih, gh, gi, grad_out, o
                     in1=by_token(n, half), op=ALU.subtract,
                 )
             nc.scalar.activation(out=n[:], in_=n[:], func=FUNC.Tanh)
-            sn = work.tile([P, H], F32, name="sn")
-            nc.scalar.activation(out=sn[:], in_=n[:], func=FUNC.Square)
             tiles["n"] = n
 
             def make_q():
@@ -244,7 +242,11 @@ def tile_grucellmodel_pa_v_kernel(tc, input_seq, W_ih, b_ih, gh, gi, grad_out, o
             else:
                 make_q()
                 make_c()
-            tiles["sn"] = sn
+
+        def square_n(t):
+            sn = work.tile([P, H], F32, name="sn")
+            nc.scalar.activation(out=sn[:], in_=live[t]["n"][:], func=FUNC.Square)
+            live[t]["sn"] = sn
 
         def last_gradients(tiles, dgi):
             nc.vector.scalar_tensor_tensor(
@@ -354,9 +356,12 @@ def tile_grucellmodel_pa_v_kernel(tc, input_seq, W_ih, b_ih, gh, gi, grad_out, o
                         transpose_n(step)
                     transpose_dh(step)
                     sigmoid(step, 0, 0)
+                if in_range(step - 1):
+                    square_n(step - 1)
+                if in_range(step):
                     sigmoid(step, 0, 1)
-                    square_r(step)
                     sigmoid(step, 1, 0)
+                    square_r(step)
                 if step == 1:
                     group_w(3)
                     group_w(4)

@@ -23,8 +23,9 @@ HALVES = H // K_PASS
 GATES = 3
 PASSES = GATES * HALVES
 EARLY_PASSES = 3
-VECTOR_DZ = 192
+VECTOR_DZ = 224
 GPSIMD_GROUPS = (3, 4)
+LAST_GATE_ORDER = (2, 0, 1)
 GATE_ORDER = (1, 2, 0)
 
 FLOPS = 2 * T * B * GATES * H * I
@@ -40,7 +41,7 @@ def tile_grucellmodel_pa_v_kernel(tc, input_seq, W_ih, b_ih, gh, gi, grad_out, o
         gi_pool = pools.enter_context(tc.tile_pool(name="gi", bufs=3))
         work = pools.enter_context(tc.tile_pool(name="work", bufs=3))
         quant = pools.enter_context(tc.tile_pool(name="quant", bufs=2))
-        result = pools.enter_context(tc.tile_pool(name="result", bufs=2))
+        result = pools.enter_context(tc.tile_pool(name="result", bufs=3))
         psum_fixed = pools.enter_context(tc.psum_pool(name="psum_fixed", bufs=1))
         psum_x = pools.enter_context(tc.psum_pool(name="psum_x", bufs=3))
         psum_an = pools.enter_context(tc.psum_pool(name="psum_an", bufs=2))
@@ -255,10 +256,11 @@ def tile_grucellmodel_pa_v_kernel(tc, input_seq, W_ih, b_ih, gh, gi, grad_out, o
             )
             nc.scalar.copy(out=dgi[:, 2, :], in_=tiles["sn"][:])
             nc.vector.tensor_tensor(out=tiles["z"][:], in0=tiles["n"][:], in1=tiles["z"][:], op=ALU.mult)
-            nc.vector.tensor_tensor(out=dgi[:, 1, :], in0=tiles["z"][:], in1=tiles["q"][:], op=ALU.mult)
-            quantise_gates(T - 1, slice(1, 3))
             nc.vector.tensor_tensor(out=dgi[:, 0, :], in0=tiles["sr"][:], in1=tiles["sn"][:], op=ALU.mult)
+            quantise_gates(T - 1, slice(2, 3))
+            nc.vector.tensor_tensor(out=dgi[:, 1, :], in0=tiles["z"][:], in1=tiles["q"][:], op=ALU.mult)
             quantise_gates(T - 1, slice(0, 1))
+            quantise_gates(T - 1, slice(1, 2))
 
         def gradients(t):
             tiles = live[t]
@@ -300,13 +302,13 @@ def tile_grucellmodel_pa_v_kernel(tc, input_seq, W_ih, b_ih, gh, gi, grad_out, o
 
         def multiply(t):
             tiles = live[t]
-            if t == T - 1:
+            if t >= T - 3:
                 x = psum_x.tile([P, PACK, B], F32, name="x")
                 acc = x[:].rearrange("p j b -> p (j b)")
             else:
                 acc_t = psum_fixed.tile([B, I], F32, name="acc")
                 acc = acc_t[:]
-            pass_order = [gate * HALVES + half for gate in GATE_ORDER for half in range(HALVES)]
+            pass_order = [gate * HALVES + half for gate in (GATE_ORDER if t < T - 1 else LAST_GATE_ORDER) for half in range(HALVES)]
             for g in pass_order:
                 gate, half = divmod(g, HALVES)
                 tokens = slice(half * B, (half + 1) * B)
@@ -360,8 +362,11 @@ def tile_grucellmodel_pa_v_kernel(tc, input_seq, W_ih, b_ih, gh, gi, grad_out, o
                     square_n(step - 1)
                 if in_range(step):
                     sigmoid(step, 0, 1)
+                    if step == 0:
+                        square_r(step)
                     sigmoid(step, 1, 0)
-                    square_r(step)
+                    if step > 0:
+                        square_r(step)
                 if step == 1:
                     group_w(3)
                     group_w(4)
@@ -376,10 +381,10 @@ def tile_grucellmodel_pa_v_kernel(tc, input_seq, W_ih, b_ih, gh, gi, grad_out, o
                     quantise_w(5)
             store(T - 4)
             multiply(T - 3)
-            store(T - 3)
             quantise(T - 2)
             multiply(T - 2)
             gradients(T - 1)
-            multiply(T - 1)
+            store(T - 3)
             store(T - 2)
+            multiply(T - 1)
             store(T - 1)

from contextlib import ExitStack

import concourse.mybir as mybir
from concourse.masks import make_identity

F32 = mybir.dt.float32
BF16 = mybir.dt.bfloat16
U32 = mybir.dt.uint32
U8 = mybir.dt.uint8
E4M3X4 = mybir.dt.float8_e4m3fn_x4
E5M2X4 = mybir.dt.float8_e5m2_x4
ALU = mybir.AluOpType
FUNC = mybir.ActivationFunctionType

T = 16
B = 128
I = 512
H = 1024
P = 128
PACK = 4
K_PASS = P * PACK
HALVES = H // K_PASS
GATES = 3
PASSES = GATES * HALVES
EARLY_PASSES = 3
VECTOR_DZ = 224
GPSIMD_GROUPS = (3, 4)
LAST_GATE_ORDER = (2, 0, 1)
GATE_ORDER = (1, 2, 0)

FLOPS = 2 * T * B * GATES * H * I
BYTES = 4 * T * B * GATES * H + 2 * B * T * H + 2 * B * GATES * H + 2 * GATES * H * I + 4 * T * B * I


def tile_grucellmodel_pa_v_kernel(tc, input_seq, W_ih, b_ih, gh, gi, grad_out, out):
    nc = tc.nc
    with ExitStack() as pools:
        const = pools.enter_context(tc.tile_pool(name="const", bufs=1))
        w_load = pools.enter_context(tc.tile_pool(name="w_load", bufs=PASSES))
        w_stage = pools.enter_context(tc.tile_pool(name="w_stage", bufs=3))
        gi_pool = pools.enter_context(tc.tile_pool(name="gi", bufs=3))
        work = pools.enter_context(tc.tile_pool(name="work", bufs=3))
        quant = pools.enter_context(tc.tile_pool(name="quant", bufs=2))
        result = pools.enter_context(tc.tile_pool(name="result", bufs=3))
        psum_fixed = pools.enter_context(tc.psum_pool(name="psum_fixed", bufs=1))
        psum_x = pools.enter_context(tc.psum_pool(name="psum_x", bufs=3))
        psum_an = pools.enter_context(tc.psum_pool(name="psum_an", bufs=2))

        w_view = W_ih.rearrange("(g j p) n -> g p j n", j=PACK, p=P)
        w_raws = []

        def load_w(g):
            w_raw = w_load.tile([P, PACK, I], BF16, name="w_raw")
            nc.sync.dma_start(out=w_raw[:], in_=w_view[g])
            w_raws.append(w_raw)

        gh_sb = const.tile([P, GATES * H], BF16)

        def load_gh(gates):
            cols = slice(gates.start * H, gates.stop * H)
            nc.sync.dma_start(out=gh_sb[:, cols], in_=gh[:, cols])

        gi_tiles = {}

        go_sb = const.tile([P, T, H], BF16)

        def load_gates(t, gates):
            if t not in gi_tiles:
                gi_t = gi_pool.tile([P, GATES * H], F32, name="gi_t")
                gi_tiles[t] = gi_t
            cols = slice(gates.start * H, gates.stop * H)
            nc.sync.dma_start(out=gi_tiles[t][:, cols], in_=gi[t][:, cols])

        def load_go(t):
            nc.sync.dma_start(out=go_sb[:, t, :], in_=grad_out[:, t, :])

        def load_step(t):
            load_gates(t, slice(0, GATES))
            load_go(t)

        for g in range(EARLY_PASSES):
            load_w(g)
        load_gh(slice(0, 1))
        load_gates(0, slice(0, 1))
        load_gh(slice(1, 3))
        load_gates(0, slice(2, 3))
        load_gates(0, slice(1, 2))
        load_go(0)
        load_w(3)
        load_gates(1, slice(0, 1))
        load_w(4)
        load_gates(1, slice(1, 3))
        load_go(1)
        load_w(5)

        ident_f32 = const.tile([P, P], F32)
        make_identity(nc, ident_f32[:])
        ident_bf16 = const.tile([P, P], BF16)
        make_identity(nc, ident_bf16[:])
        minus_half = const.tile([P, 1], F32)
        nc.vector.memset(minus_half[:], -0.5)

        g_rz = const.tile([P, 2 * H], F32)
        neg_hn = const.tile([P, H], BF16)

        def transpose_bf16(dst, src):
            for half in range(HALVES):
                for j in range(PACK):
                    blk = half * PACK + j
                    nc.tensor.transpose(
                        dst[:, j, half * B : (half + 1) * B], src[:, blk * P : (blk + 1) * P], ident_bf16[:]
                    )

        neg_hn_t = psum_fixed.tile([P, PACK, HALVES * B], BF16)

        w_codes = const.tile([P, PASSES, I], U32, align_bytes=64)
        w_scales = const.tile([P, PASSES, I], U8, align_bytes=64)
        w_grouped = {}

        def group_w(g):
            w_grp = w_stage.tile([P, I, PACK], BF16, name="w_grp", align_bytes=64)
            if g in GPSIMD_GROUPS:
                nc.gpsimd.tensor_scalar(
                    out=w_grp[:], in0=w_raws[g][:].rearrange("p j n -> p n j"),
                    scalar1=1.0, scalar2=0.0, op0=ALU.mult, op1=ALU.add,
                )
            else:
                nc.vector.tensor_copy(
                    out=w_grp[:].rearrange("p (c i) j -> p c j i", i=4),
                    in_=w_raws[g][:].rearrange("p j (c i) -> p c j i", i=4),
                )
            w_grouped[g] = w_grp

        def quantise_w(g):
            nc.vector.quantize_mx(
                out=w_codes[:, g, :].bitcast(E4M3X4),
                scales=w_scales[:, g, :],
                in_=w_grouped[g][:].rearrange("p n j -> p (n j)"),
            )

        group_w(0)
        group_w(1)
        quantise_w(0)
        nc.vector.tensor_copy(out=g_rz[:, 0:H], in_=gh_sb[:, 0:H])
        group_w(2)
        quantise_w(1)
        nc.vector.tensor_scalar(
            out=neg_hn[:], in0=gh_sb[:, 2 * H : 3 * H], scalar1=-1.0, scalar2=None, op0=ALU.mult
        )
        nc.vector.tensor_copy(out=g_rz[:, H:], in_=gh_sb[:, H : 2 * H])
        quantise_w(2)

        live = {}

        def by_token(flat, half):
            return flat[:, half * K_PASS : (half + 1) * K_PASS].rearrange("p (b j) -> p b j", j=PACK)

        def all_tokens(flat):
            return flat[:].rearrange("p (c j) -> p c j", j=PACK)

        def transpose_gate(t, gate, half):
            x = psum_x.tile([P, PACK, B], F32, name="x")
            for j in range(PACK):
                cols = slice(gate * H + half * K_PASS + j * P, gate * H + half * K_PASS + (j + 1) * P)
                nc.tensor.matmul(
                    x[:, j, :], lhsT=gi_tiles[t][:, cols], rhs=ident_f32[:],
                    is_transpose=True, start=True, stop=False,
                )
                nc.tensor.matmul(
                    x[:, j, :], lhsT=g_rz[:, cols], rhs=ident_f32[:],
                    is_transpose=True, start=False, stop=True,
                )
            live.setdefault(t, {})[("x", gate, half)] = x

        def sigmoid(t, gate, half):
            tiles = live[t]
            name = ("r", "z")[gate]
            if half == 0:
                if gate == 0:
                    r = work.tile([P, H], F32, name="r")
                    tiles["r"] = r
                else:
                    z = work.tile([P, H], F32, name="z")
                    tiles["z"] = z
            nc.scalar.activation(
                out=by_token(tiles[name], half), in_=tiles[("x", gate, half)][:].rearrange("p j b -> p b j"),
                func=FUNC.Sigmoid,
            )

        def square_r(t):
            sr = work.tile([P, H], F32, name="sr")
            nc.scalar.activation(out=sr[:], in_=live[t]["r"][:], func=FUNC.Square, bias=minus_half[:], scale=1.0)
            live[t]["sr"] = sr

        def transpose_n(t):
            a_n = []
            for half in range(HALVES):
                a_half = psum_an.tile([P, PACK, B], F32, name="a_half")
                for j in range(PACK):
                    cols = slice(2 * H + half * K_PASS + j * P, 2 * H + half * K_PASS + (j + 1) * P)
                    nc.tensor.transpose(a_half[:, j, :], gi_tiles[t][:, cols], ident_f32[:])
                a_n.append(a_half)
            live[t]["a_n"] = a_n

        def transpose_dh(t):
            dh_t = psum_fixed.tile([P, PACK, HALVES * B], BF16, name="dh_t")
            transpose_bf16(dh_t, go_sb[:, t, :])
            live[t]["dh_t"] = dh_t

        def gate_n(t):
            tiles = live[t]
            n = work.tile([P, H], F32, name="n")
            for half in range(HALVES):
                nc.vector.tensor_tensor(
                    out=by_token(n, half), in0=by_token(tiles["r"], half),
                    in1=neg_hn_t[:, :, half * B : (half + 1) * B].rearrange("p j b -> p b j"), op=ALU.mult,
                )
            for half in range(HALVES):
                nc.vector.tensor_tensor(
                    out=by_token(n, half), in0=tiles["a_n"][half][:].rearrange("p j b -> p b j"),
                    in1=by_token(n, half), op=ALU.subtract,
                )
            nc.scalar.activation(out=n[:], in_=n[:], func=FUNC.Tanh)
            tiles["n"] = n

            def make_q():
                q = work.tile([P, H], F32, name="q")
                nc.vector.scalar_tensor_tensor(
                    out=all_tokens(q), in0=all_tokens(tiles["z"]), scalar=1.0,
                    in1=tiles["dh_t"][:].rearrange("p j c -> p c j"), op0=ALU.subtract, op1=ALU.mult,
                )
                tiles["q"] = q

            def make_c():
                nc.vector.scalar_tensor_tensor(
                    out=all_tokens(tiles["sr"]), in0=all_tokens(tiles["sr"]), scalar=0.25,
                    in1=neg_hn_t[:].rearrange("p j c -> p c j"), op0=ALU.subtract, op1=ALU.mult,
                )

            if t == 0:
                make_c()
                make_q()
            else:
                make_q()
                make_c()

        def square_n(t):
            sn = work.tile([P, H], F32, name="sn")
            nc.scalar.activation(out=sn[:], in_=live[t]["n"][:], func=FUNC.Square)
            live[t]["sn"] = sn

        def last_gradients(tiles, dgi):
            nc.vector.scalar_tensor_tensor(
                out=tiles["sn"][:], in0=tiles["sn"][:], scalar=1.0, in1=tiles["q"][:],
                op0=ALU.subtract, op1=ALU.mult,
            )
            nc.scalar.copy(out=dgi[:, 2, :], in_=tiles["sn"][:])
            nc.vector.tensor_tensor(out=tiles["z"][:], in0=tiles["n"][:], in1=tiles["z"][:], op=ALU.mult)
            nc.vector.tensor_tensor(out=dgi[:, 0, :], in0=tiles["sr"][:], in1=tiles["sn"][:], op=ALU.mult)
            quantise_gates(T - 1, slice(2, 3))
            nc.vector.tensor_tensor(out=dgi[:, 1, :], in0=tiles["z"][:], in1=tiles["q"][:], op=ALU.mult)
            quantise_gates(T - 1, slice(0, 1))
            quantise_gates(T - 1, slice(1, 2))

        def gradients(t):
            tiles = live[t]
            tiles["dgi"] = dgi = quant.tile([P, GATES, H], BF16, name="dgi", align_bytes=64)
            if t == T - 1:
                last_gradients(tiles, dgi)
                return
            nc.vector.tensor_tensor(out=tiles["z"][:], in0=tiles["n"][:], in1=tiles["z"][:], op=ALU.mult)
            nc.vector.scalar_tensor_tensor(
                out=tiles["sn"][:], in0=tiles["sn"][:], scalar=1.0, in1=tiles["q"][:],
                op0=ALU.subtract, op1=ALU.mult,
            )
            split = VECTOR_DZ
            nc.vector.tensor_tensor(
                out=dgi[:, 1, :split], in0=tiles["z"][:, :split], in1=tiles["q"][:, :split], op=ALU.mult
            )
            nc.gpsimd.tensor_tensor(out=dgi[:, 0, :], in0=tiles["sr"][:], in1=tiles["sn"][:], op=ALU.mult)
            nc.gpsimd.tensor_tensor(
                out=dgi[:, 1, split:], in0=tiles["z"][:, split:], in1=tiles["q"][:, split:], op=ALU.mult
            )
            nc.scalar.copy(out=dgi[:, 2, :], in_=tiles["sn"][:])

        def quantise_gates(t, gates):
            tiles = live[t]
            if "codes" not in tiles:
                codes = quant.tile([P, GATES, H // PACK], U32, name="codes", align_bytes=64)
                scales = quant.tile([P, GATES, H // PACK], U8, name="scales", align_bytes=64)
                tiles["codes"] = codes
                tiles["scales"] = scales
            nc.vector.quantize_mx(
                out=tiles["codes"][:, gates, :].rearrange("p g c -> p (g c)").bitcast(E5M2X4),
                scales=tiles["scales"][:, gates, :].rearrange("p g c -> p (g c)"),
                in_=tiles["dgi"][:, gates, :].rearrange("p g c -> p (g c)"),
            )

        def quantise(t):
            quantise_gates(t, slice(1, 3))
            quantise_gates(t, slice(0, 1))

        def multiply(t):
            tiles = live[t]
            if t >= T - 3:
                x = psum_x.tile([P, PACK, B], F32, name="x")
                acc = x[:].rearrange("p j b -> p (j b)")
            else:
                acc_t = psum_fixed.tile([B, I], F32, name="acc")
                acc = acc_t[:]
            pass_order = [gate * HALVES + half for gate in (GATE_ORDER if t < T - 1 else LAST_GATE_ORDER) for half in range(HALVES)]
            for g in pass_order:
                gate, half = divmod(g, HALVES)
                tokens = slice(half * B, (half + 1) * B)
                nc.tensor.matmul_mx(
                    out=acc,
                    lhsT=tiles["codes"][:, gate, tokens].bitcast(E5M2X4),
                    lhsT_scale=tiles["scales"][:, gate, tokens],
                    rhs=w_codes[:, g, :].bitcast(E4M3X4),
                    rhs_scale=w_scales[:, g, :],
                    start=(g == pass_order[0]),
                    stop=(g == pass_order[-1]),
                )
            tiles["acc"] = acc

        def store(t):
            o_sb = result.tile([B, I], F32, name="o_sb")
            nc.scalar.copy(out=o_sb[:], in_=live[t]["acc"])
            nc.sync.dma_start(out=out[t], in_=o_sb[:])

        def in_range(t):
            return 0 <= t < T

        with tc.manual_schedule():
            for step in range(T + 1):
                if in_range(step - 1):
                    transpose_gate(step - 1, 1, 1)
                    sigmoid(step - 1, 1, 1)
                if in_range(step + 2):
                    load_step(step + 2)
                if in_range(step):
                    transpose_gate(step, 0, 0)
                    transpose_gate(step, 0, 1)
                    if step == 0:
                        transpose_bf16(neg_hn_t, neg_hn)
                        transpose_n(step)
                    transpose_gate(step, 1, 0)
                if in_range(step - 5):
                    store(step - 5)
                if in_range(step - 4):
                    multiply(step - 4)
                if in_range(step - 2):
                    gradients(step - 2)
                if in_range(step - 1):
                    gate_n(step - 1)
                if in_range(step):
                    if step > 0:
                        transpose_n(step)
                    transpose_dh(step)
                    sigmoid(step, 0, 0)
                if in_range(step - 1):
                    square_n(step - 1)
                if in_range(step):
                    sigmoid(step, 0, 1)
                    if step == 0:
                        square_r(step)
                    sigmoid(step, 1, 0)
                    if step > 0:
                        square_r(step)
                if step == 1:
                    group_w(3)
                    group_w(4)
                if step == 2:
                    group_w(5)
                    quantise_w(3)
                if step == 3:
                    quantise_w(4)
                if in_range(step - 3):
                    quantise(step - 3)
                if step == 3:
                    quantise_w(5)
            store(T - 4)
            multiply(T - 3)
            quantise(T - 2)
            multiply(T - 2)
            gradients(T - 1)
            store(T - 3)
            store(T - 2)
            multiply(T - 1)
            store(T - 1)
